import numpy as np
import ml_dtypes

BF16 = ml_dtypes.bfloat16


def bf(x):
    return np.asarray(x, np.float32).astype(BF16)


def f32(x):
    return np.asarray(x, np.float32)


def f64(x):
    return np.asarray(x).astype(np.float64)


def striped(idx):
    return np.tile(idx.reshape(-1, 16).T, (8, 1))


C, S, N, K = 512, 4096, 1024, 3
PERIODS = (86400.0, 604800.0, 2592000.0)
TMAX = 40000.0


def setup_inputs():
    return {'table': f32(np.random.standard_normal((C, S)) / np.sqrt(C)), 'time_seq': f32(TMAX * np.random.random((1, N))), 'time_proj': f32(0.4 * np.random.standard_normal((C, 2 * K))), 'offs': striped(np.random.permutation(np.tile(np.arange(S), 2))[:N])}


def reference(table, time_seq, time_proj, offs):
    idx = offs[:16].T.reshape(-1)
    emb = np.sqrt(C) * f64(table)
    te = np.zeros((C, N))
    for k in range(K):
        phase = 2.0 * np.pi * f64(time_seq) / PERIODS[k]
        te = te + f64(time_proj)[:, k:k + 1] * np.sin(phase) + f64(time_proj)[:, K + k:K + k + 1] * np.cos(phase)
    return emb[:, idx] + te

@@ -1,0 +1,96 @@
+import math
+
+import concourse.mybir as mybir
+from concourse.masks import make_identity
+
+F32 = mybir.dt.float32
+I32 = mybir.dt.int32
+U16 = mybir.dt.uint16
+ALU = mybir.AluOpType
+ACT = mybir.ActivationFunctionType
+
+P = 128
+C, S, N, K = 512, 4096, 1024, 3
+PERIODS = (86400.0, 604800.0, 2592000.0)
+ROWS = 2 * K
+BLOCKS = C // P
+BANK = 512
+CHUNK = 1024
+
+FLOPS = 2 * C * N * ROWS
+
+
+def tile_cyclictisasrec_kernel(tc, table, time_seq, time_proj, offs, out):
+    nc = tc.nc
+    with (
+        tc.tile_pool(name="held", bufs=1) as held,
+        tc.psum_pool(name="flip", bufs=1) as flip,
+        tc.psum_pool(name="banks", bufs=4) as banks,
+    ):
+        offsets = held.tile([P, N // 16], U16, name="offsets")
+        nc.sync.dma_start(offsets[:], offs)
+
+        stamps = held.tile([ROWS, N], F32, name="stamps")
+        nc.scalar.dma_start(stamps[:], time_seq.broadcast_to([ROWS, N]))
+        proj = held.tile([P, BLOCKS, ROWS], F32, name="proj")
+        nc.scalar.dma_start(proj[:], time_proj.rearrange("(b p) r -> p b r", p=P))
+
+        raw = [held.tile([P, S], F32, name=f"raw{b}") for b in range(BLOCKS)]
+        for b in range(BLOCKS):
+            for first in range(0, S, CHUNK):
+                nc.sync.dma_start(
+                    raw[b][:, first : first + CHUNK],
+                    table[b * P : (b + 1) * P, first : first + CHUNK],
+                )
+
+        rate = held.tile([ROWS, 1], F32, name="rate")
+        for r in reversed(range(ROWS)):
+            nc.gpsimd.memset(rate[0 : r + 1, :], 1.0 / PERIODS[r % K])
+        lead = held.tile([ROWS, 1], F32, name="lead")
+        nc.gpsimd.memset(lead[:], 0.25)
+        nc.gpsimd.memset(lead[0:K, :], 0.0)
+
+        turns = held.tile([ROWS, N], F32, name="turns")
+        nc.vector.tensor_scalar(turns[:], stamps[:], rate[:, 0:1], lead[:, 0:1], ALU.mult, ALU.add)
+        whole = held.tile([ROWS, N], I32, name="whole")
+        nc.vector.tensor_copy(whole[:], turns[:])
+        part = held.tile([ROWS, N], F32, name="part")
+        nc.vector.tensor_tensor(part[:], turns[:], whole[:], ALU.subtract)
+
+        harmonics = held.tile([P, N], F32, name="harmonics")
+        nc.gpsimd.memset(harmonics[:], 0.0)
+        nc.scalar.activation(harmonics[0:ROWS, :], part[:], ACT.Sin, scale=2.0 * math.pi)
+
+        identity = held.tile([P, P], F32, name="identity")
+        make_identity(nc, identity[:])
+        flipped = flip.tile([ROWS, C], F32, name="flipped")
+        for b in range(BLOCKS):
+            nc.tensor.transpose(flipped[:, b * P : (b + 1) * P], proj[:, b, :], identity[:])
+        weights = held.tile([P, C], F32, name="weights")
+        nc.gpsimd.memset(weights[:], 0.0)
+        nc.vector.tensor_copy(weights[0:ROWS, :], flipped[:])
+
+        for b in range(BLOCKS):
+            te = held.tile([P, N], F32, name=f"te{b}")
+            for first in range(0, N, BANK):
+                product = banks.tile([P, BANK], F32, name="product")
+                nc.tensor.matmul(
+                    product[:],
+                    weights[:, b * P : (b + 1) * P],
+                    harmonics[:, first : first + BANK],
+                    start=True,
+                    stop=True,
+                )
+                nc.scalar.copy(te[:, first : first + BANK], product[:])
+
+            emb = held.tile([P, S], F32, name=f"emb{b}")
+            for q, first in enumerate(range(0, S, CHUNK)):
+                chunk = slice(first, first + CHUNK)
+                if q % 2 == 0:
+                    nc.scalar.mul(emb[:, chunk], raw[b][:, chunk], math.sqrt(C))
+                else:
+                    nc.vector.tensor_scalar_mul(emb[:, chunk], raw[b][:, chunk], math.sqrt(C))
+
+            summed = held.tile([P, N], F32, name=f"summed{b}")
+            nc.vector.tensor_tensor(summed[:], emb[:].indirect(offsets[:]), te[:], ALU.add)
+            nc.sync.dma_start(out[b * P : (b + 1) * P, :], summed[:])

@@ -14,6 +14,7 @@ C, S, N, K = 512, 4096, 1024, 3
 PERIODS = (86400.0, 604800.0, 2592000.0)
 ROWS = 2 * K
 BLOCKS = C // P
+GROUPS = N // P
 BANK = 512
 CHUNK = 1024
 
@@ -22,58 +23,70 @@ FLOPS = 2 * C * N * ROWS
 
 def tile_cyclictisasrec_kernel(tc, table, time_seq, time_proj, offs, out):
     nc = tc.nc
+    table_blocks = table.rearrange("(p b) s -> b p s", b=BLOCKS)
+    out_blocks = out.rearrange("(p b) n -> b p n", b=BLOCKS)
     with (
         tc.tile_pool(name="held", bufs=1) as held,
-        tc.psum_pool(name="flip", bufs=1) as flip,
-        tc.psum_pool(name="banks", bufs=4) as banks,
+        tc.psum_pool(name="banks", bufs=8) as banks,
     ):
         offsets = held.tile([P, N // 16], U16, name="offsets")
         nc.sync.dma_start(offsets[:], offs)
 
-        stamps = held.tile([ROWS, N], F32, name="stamps")
-        nc.scalar.dma_start(stamps[:], time_seq.broadcast_to([ROWS, N]))
+        stamp_rows = held.tile([P, P], F32, name="stamp_rows")
+        nc.gpsimd.memset(stamp_rows[:], 0.0)
+        nc.sync.dma_start(stamp_rows[0:GROUPS, :], time_seq.rearrange("o (g p) -> (o g) p", p=P))
         proj = held.tile([P, BLOCKS, ROWS], F32, name="proj")
-        nc.scalar.dma_start(proj[:], time_proj.rearrange("(b p) r -> p b r", p=P))
+        nc.sync.dma_start(proj[:], time_proj.rearrange("(p b) r -> p b r", b=BLOCKS))
 
         raw = [held.tile([P, S], F32, name=f"raw{b}") for b in range(BLOCKS)]
         for b in range(BLOCKS):
             for first in range(0, S, CHUNK):
                 nc.sync.dma_start(
-                    raw[b][:, first : first + CHUNK],
-                    table[b * P : (b + 1) * P, first : first + CHUNK],
+                    raw[b][:, first : first + CHUNK], table_blocks[b, :, first : first + CHUNK]
                 )
-
-        rate = held.tile([ROWS, 1], F32, name="rate")
-        for r in reversed(range(ROWS)):
-            nc.gpsimd.memset(rate[0 : r + 1, :], 1.0 / PERIODS[r % K])
-        lead = held.tile([ROWS, 1], F32, name="lead")
-        nc.gpsimd.memset(lead[:], 0.25)
-        nc.gpsimd.memset(lead[0:K, :], 0.0)
-
-        turns = held.tile([ROWS, N], F32, name="turns")
-        nc.vector.tensor_scalar(turns[:], stamps[:], rate[:, 0:1], lead[:, 0:1], ALU.mult, ALU.add)
-        whole = held.tile([ROWS, N], I32, name="whole")
-        nc.vector.tensor_copy(whole[:], turns[:])
-        part = held.tile([ROWS, N], F32, name="part")
-        nc.vector.tensor_tensor(part[:], turns[:], whole[:], ALU.subtract)
-
-        harmonics = held.tile([P, N], F32, name="harmonics")
-        nc.gpsimd.memset(harmonics[:], 0.0)
-        nc.scalar.activation(harmonics[0:ROWS, :], part[:], ACT.Sin, scale=2.0 * math.pi)
 
         identity = held.tile([P, P], F32, name="identity")
         make_identity(nc, identity[:])
-        flipped = flip.tile([ROWS, C], F32, name="flipped")
+
+        stamps = banks.tile([P, P], F32, name="bank")
+        nc.tensor.transpose(stamps[:], stamp_rows[:], identity[:])
+
+        turns = held.tile([P, ROWS, GROUPS], F32, name="turns")
+        for k in range(K):
+            nc.vector.tensor_scalar_mul(turns[:, k, :], stamps[:, 0:GROUPS], 1.0 / PERIODS[k])
+        nc.vector.tensor_scalar_add(turns[:, K:ROWS, :], turns[:, 0:K, :], 0.25)
+
+        whole = held.tile([P, ROWS, GROUPS], I32, name="whole")
+        nc.vector.tensor_copy(whole[:], turns[:])
+        part = held.tile([P, ROWS, GROUPS], F32, name="part")
+        nc.vector.tensor_tensor(part[:], turns[:], whole[:], ALU.subtract)
+
+        waves = held.tile([P, GROUPS, ROWS], F32, name="waves")
+        nc.scalar.activation(
+            waves[:], part[:].rearrange("p r g -> p g r"), ACT.Sin, scale=2.0 * math.pi
+        )
+
+        harmonics = held.tile([P, N], F32, name="harmonics")
+        nc.gpsimd.memset(harmonics[:], 0.0)
+        for first in range(0, N, BANK):
+            flat = banks.tile([ROWS, BANK], F32, name="bank")
+            for g in range(BANK // P):
+                nc.tensor.transpose(
+                    flat[:, g * P : (g + 1) * P], waves[:, first // P + g, :], identity[:]
+                )
+            nc.vector.tensor_copy(harmonics[0:ROWS, first : first + BANK], flat[:])
+
+        flipped = banks.tile([ROWS, C], F32, name="bank")
         for b in range(BLOCKS):
             nc.tensor.transpose(flipped[:, b * P : (b + 1) * P], proj[:, b, :], identity[:])
         weights = held.tile([P, C], F32, name="weights")
         nc.gpsimd.memset(weights[:], 0.0)
-        nc.vector.tensor_copy(weights[0:ROWS, :], flipped[:])
+        nc.scalar.copy(weights[0:ROWS, :], flipped[:])
 
         for b in range(BLOCKS):
             te = held.tile([P, N], F32, name=f"te{b}")
             for first in range(0, N, BANK):
-                product = banks.tile([P, BANK], F32, name="product")
+                product = banks.tile([P, BANK], F32, name="bank")
                 nc.tensor.matmul(
                     product[:],
                     weights[:, b * P : (b + 1) * P],
@@ -81,16 +94,18 @@ def tile_cyclictisasrec_kernel(tc, table, time_seq, time_proj, offs, out):
                     start=True,
                     stop=True,
                 )
-                nc.scalar.copy(te[:, first : first + BANK], product[:])
+                nc.vector.tensor_copy(te[:, first : first + BANK], product[:])
 
             emb = held.tile([P, S], F32, name=f"emb{b}")
             for q, first in enumerate(range(0, S, CHUNK)):
                 chunk = slice(first, first + CHUNK)
-                if q % 2 == 0:
+                if q % 4 < 3:
                     nc.scalar.mul(emb[:, chunk], raw[b][:, chunk], math.sqrt(C))
                 else:
-                    nc.vector.tensor_scalar_mul(emb[:, chunk], raw[b][:, chunk], math.sqrt(C))
+                    nc.gpsimd.tensor_scalar(
+                        emb[:, chunk], raw[b][:, chunk], math.sqrt(C), 0.0, ALU.mult, ALU.add
+                    )
 
             summed = held.tile([P, N], F32, name=f"summed{b}")
             nc.vector.tensor_tensor(summed[:], emb[:].indirect(offsets[:]), te[:], ALU.add)
-            nc.sync.dma_start(out[b * P : (b + 1) * P, :], summed[:])
+            nc.sync.dma_start(out_blocks[b], summed[:])

@@ -7,7 +7,6 @@ F32 = mybir.dt.float32
 I32 = mybir.dt.int32
 U16 = mybir.dt.uint16
 ALU = mybir.AluOpType
-ACT = mybir.ActivationFunctionType
 
 P = 128
 C, S, N, K = 512, 4096, 1024, 3
@@ -17,6 +16,7 @@ BLOCKS = C // P
 GROUPS = N // P
 BANK = 512
 CHUNK = 1024
+SINE_TERMS = 8
 
 FLOPS = 2 * C * N * ROWS
 
@@ -51,20 +51,27 @@ def tile_cyclictisasrec_kernel(tc, table, time_seq, time_proj, offs, out):
         stamps = banks.tile([P, P], F32, name="bank")
         nc.tensor.transpose(stamps[:], stamp_rows[:], identity[:])
 
-        turns = held.tile([P, ROWS, GROUPS], F32, name="turns")
+        turns = held.tile([P, GROUPS, ROWS], F32, name="turns")
         for k in range(K):
-            nc.vector.tensor_scalar_mul(turns[:, k, :], stamps[:, 0:GROUPS], 1.0 / PERIODS[k])
-        nc.vector.tensor_scalar_add(turns[:, K:ROWS, :], turns[:, 0:K, :], 0.25)
+            nc.vector.tensor_scalar_mul(turns[:, :, k], stamps[:, 0:GROUPS], 1.0 / PERIODS[k])
+        nc.vector.tensor_scalar_add(turns[:, :, K:ROWS], turns[:, :, 0:K], 0.25)
 
-        whole = held.tile([P, ROWS, GROUPS], I32, name="whole")
+        whole = held.tile([P, GROUPS, ROWS], I32, name="whole")
         nc.vector.tensor_copy(whole[:], turns[:])
-        part = held.tile([P, ROWS, GROUPS], F32, name="part")
+        part = held.tile([P, GROUPS, ROWS], F32, name="part")
         nc.vector.tensor_tensor(part[:], turns[:], whole[:], ALU.subtract)
 
+        series = [2.0 * math.pi]
+        for i in range(1, SINE_TERMS):
+            series.append(-series[-1] * (2.0 * math.pi) ** 2 / ((2 * i) * (2 * i + 1)))
+        square = held.tile([P, GROUPS, ROWS], F32, name="square")
+        nc.vector.tensor_tensor(square[:], part[:], part[:], ALU.mult)
+        bracket = held.tile([P, GROUPS, ROWS], F32, name="bracket")
+        nc.vector.tensor_scalar_mul(bracket[:], square[:], series[-1])
+        for c in reversed(series[1:-1]):
+            nc.vector.scalar_tensor_tensor(bracket[:], bracket[:], c, square[:], ALU.add, ALU.mult)
         waves = held.tile([P, GROUPS, ROWS], F32, name="waves")
-        nc.scalar.activation(
-            waves[:], part[:].rearrange("p r g -> p g r"), ACT.Sin, scale=2.0 * math.pi
-        )
+        nc.vector.scalar_tensor_tensor(waves[:], bracket[:], series[0], part[:], ALU.add, ALU.mult)
 
         harmonics = held.tile([P, N], F32, name="harmonics")
         nc.gpsimd.memset(harmonics[:], 0.0)
@@ -81,7 +88,7 @@ def tile_cyclictisasrec_kernel(tc, table, time_seq, time_proj, offs, out):
             nc.tensor.transpose(flipped[:, b * P : (b + 1) * P], proj[:, b, :], identity[:])
         weights = held.tile([P, C], F32, name="weights")
         nc.gpsimd.memset(weights[:], 0.0)
-        nc.scalar.copy(weights[0:ROWS, :], flipped[:])
+        nc.vector.tensor_copy(weights[0:ROWS, :], flipped[:])
 
         for b in range(BLOCKS):
             te = held.tile([P, N], F32, name=f"te{b}")

@@ -4,19 +4,18 @@ import concourse.mybir as mybir
 from concourse.masks import make_identity
 
 F32 = mybir.dt.float32
-I32 = mybir.dt.int32
 U16 = mybir.dt.uint16
 ALU = mybir.AluOpType
+SIN = mybir.ActivationFunctionType.Sin
 
 P = 128
 C, S, N, K = 512, 4096, 1024, 3
 PERIODS = (86400.0, 604800.0, 2592000.0)
 ROWS = 2 * K
 BLOCKS = C // P
-GROUPS = N // P
+WAVES = 8
 BANK = 512
 CHUNK = 1024
-SINE_TERMS = 8
 
 FLOPS = 2 * C * N * ROWS
 
@@ -32,9 +31,8 @@ def tile_cyclictisasrec_kernel(tc, table, time_seq, time_proj, offs, out):
         offsets = held.tile([P, N // 16], U16, name="offsets")
         nc.sync.dma_start(offsets[:], offs)
 
-        stamp_rows = held.tile([P, P], F32, name="stamp_rows")
-        nc.gpsimd.memset(stamp_rows[:], 0.0)
-        nc.sync.dma_start(stamp_rows[0:GROUPS, :], time_seq.rearrange("o (g p) -> (o g) p", p=P))
+        stamps = held.tile([WAVES, N], F32, name="stamps")
+        nc.sync.dma_start(stamps[:], time_seq.rearrange("o n -> (o n)").partition_broadcast(WAVES))
         proj = held.tile([P, BLOCKS, ROWS], F32, name="proj")
         nc.sync.dma_start(proj[:], time_proj.rearrange("(p b) r -> p b r", b=BLOCKS))
 
@@ -48,40 +46,18 @@ def tile_cyclictisasrec_kernel(tc, table, time_seq, time_proj, offs, out):
         identity = held.tile([P, P], F32, name="identity")
         make_identity(nc, identity[:])
 
-        stamps = banks.tile([P, P], F32, name="bank")
-        nc.tensor.transpose(stamps[:], stamp_rows[:], identity[:])
-
-        turns = held.tile([P, GROUPS, ROWS], F32, name="turns")
-        for k in range(K):
-            nc.vector.tensor_scalar_mul(turns[:, :, k], stamps[:, 0:GROUPS], 1.0 / PERIODS[k])
-        nc.vector.tensor_scalar_add(turns[:, :, K:ROWS], turns[:, :, 0:K], 0.25)
-
-        whole = held.tile([P, GROUPS, ROWS], I32, name="whole")
-        nc.vector.tensor_copy(whole[:], turns[:])
-        part = held.tile([P, GROUPS, ROWS], F32, name="part")
-        nc.vector.tensor_tensor(part[:], turns[:], whole[:], ALU.subtract)
-
-        series = [2.0 * math.pi]
-        for i in range(1, SINE_TERMS):
-            series.append(-series[-1] * (2.0 * math.pi) ** 2 / ((2 * i) * (2 * i + 1)))
-        square = held.tile([P, GROUPS, ROWS], F32, name="square")
-        nc.vector.tensor_tensor(square[:], part[:], part[:], ALU.mult)
-        bracket = held.tile([P, GROUPS, ROWS], F32, name="bracket")
-        nc.vector.tensor_scalar_mul(bracket[:], square[:], series[-1])
-        for c in reversed(series[1:-1]):
-            nc.vector.scalar_tensor_tensor(bracket[:], bracket[:], c, square[:], ALU.add, ALU.mult)
-        waves = held.tile([P, GROUPS, ROWS], F32, name="waves")
-        nc.vector.scalar_tensor_tensor(waves[:], bracket[:], series[0], part[:], ALU.add, ALU.mult)
-
+        rate = held.tile([WAVES, 1], F32, name="rate")
+        shift = held.tile([WAVES, 1], F32, name="shift")
+        nc.vector.memset(rate[:], 0.0)
+        for r in reversed(range(ROWS)):
+            turn = 2.0 * math.pi if r < K else -2.0 * math.pi
+            nc.vector.memset(rate[0 : r + 1, :], turn / PERIODS[r % K])
+        nc.vector.memset(shift[:], 0.0)
+        nc.vector.memset(shift[0:ROWS, :], math.pi / 2.0)
+        nc.vector.memset(shift[0:K, :], 0.0)
         harmonics = held.tile([P, N], F32, name="harmonics")
         nc.gpsimd.memset(harmonics[:], 0.0)
-        for first in range(0, N, BANK):
-            flat = banks.tile([ROWS, BANK], F32, name="bank")
-            for g in range(BANK // P):
-                nc.tensor.transpose(
-                    flat[:, g * P : (g + 1) * P], waves[:, first // P + g, :], identity[:]
-                )
-            nc.vector.tensor_copy(harmonics[0:ROWS, first : first + BANK], flat[:])
+        nc.scalar.activation(harmonics[0:WAVES, :], stamps[:], SIN, bias=shift[:], scale=rate[:])
 
         flipped = banks.tile([ROWS, C], F32, name="bank")
         for b in range(BLOCKS):
@@ -90,8 +66,8 @@ def tile_cyclictisasrec_kernel(tc, table, time_seq, time_proj, offs, out):
         nc.gpsimd.memset(weights[:], 0.0)
         nc.vector.tensor_copy(weights[0:ROWS, :], flipped[:])
 
+        te = [held.tile([P, N], F32, name=f"te{b}") for b in range(BLOCKS)]
         for b in range(BLOCKS):
-            te = held.tile([P, N], F32, name=f"te{b}")
             for first in range(0, N, BANK):
                 product = banks.tile([P, BANK], F32, name="bank")
                 nc.tensor.matmul(
@@ -101,8 +77,9 @@ def tile_cyclictisasrec_kernel(tc, table, time_seq, time_proj, offs, out):
                     start=True,
                     stop=True,
                 )
-                nc.vector.tensor_copy(te[:, first : first + BANK], product[:])
+                nc.vector.tensor_copy(te[b][:, first : first + BANK], product[:])
 
+        for b in range(BLOCKS):
             emb = held.tile([P, S], F32, name=f"emb{b}")
             for q, first in enumerate(range(0, S, CHUNK)):
                 chunk = slice(first, first + CHUNK)
@@ -114,5 +91,5 @@ def tile_cyclictisasrec_kernel(tc, table, time_seq, time_proj, offs, out):
                     )
 
             summed = held.tile([P, N], F32, name=f"summed{b}")
-            nc.vector.tensor_tensor(summed[:], emb[:].indirect(offsets[:]), te[:], ALU.add)
+            nc.vector.tensor_tensor(summed[:], emb[:].indirect(offsets[:]), te[b][:], ALU.add)
             nc.sync.dma_start(out_blocks[b], summed[:])

@@ -16,6 +16,7 @@ BLOCKS = C // P
 WAVES = 8
 BANK = 512
 CHUNK = 1024
+PIECE = 512
 
 FLOPS = 2 * C * N * ROWS
 
@@ -36,12 +37,12 @@ def tile_cyclictisasrec_kernel(tc, table, time_seq, time_proj, offs, out):
         proj = held.tile([P, BLOCKS, ROWS], F32, name="proj")
         nc.sync.dma_start(proj[:], time_proj.rearrange("(p b) r -> p b r", b=BLOCKS))
 
+        chunks = [[slice(first, first + CHUNK) for first in range(0, S, CHUNK)] for b in range(BLOCKS)]
+        chunks[-1][-1:] = [slice(S - CHUNK, S - CHUNK // 2), slice(S - CHUNK // 2, S)]
         raw = [held.tile([P, S], F32, name=f"raw{b}") for b in range(BLOCKS)]
         for b in range(BLOCKS):
-            for first in range(0, S, CHUNK):
-                nc.sync.dma_start(
-                    raw[b][:, first : first + CHUNK], table_blocks[b, :, first : first + CHUNK]
-                )
+            for chunk in chunks[b]:
+                nc.sync.dma_start(raw[b][:, chunk], table_blocks[b, :, chunk])
 
         identity = held.tile([P, P], F32, name="identity")
         make_identity(nc, identity[:])
@@ -81,15 +82,21 @@ def tile_cyclictisasrec_kernel(tc, table, time_seq, time_proj, offs, out):
 
         for b in range(BLOCKS):
             emb = held.tile([P, S], F32, name=f"emb{b}")
-            for q, first in enumerate(range(0, S, CHUNK)):
-                chunk = slice(first, first + CHUNK)
-                if q % 4 < 3:
-                    nc.scalar.mul(emb[:, chunk], raw[b][:, chunk], math.sqrt(C))
-                else:
+            for q, chunk in enumerate(chunks[b]):
+                if q == 2:
                     nc.gpsimd.tensor_scalar(
                         emb[:, chunk], raw[b][:, chunk], math.sqrt(C), 0.0, ALU.mult, ALU.add
                     )
+                else:
+                    nc.scalar.mul(emb[:, chunk], raw[b][:, chunk], math.sqrt(C))
 
             summed = held.tile([P, N], F32, name=f"summed{b}")
-            nc.vector.tensor_tensor(summed[:], emb[:].indirect(offsets[:]), te[b][:], ALU.add)
-            nc.sync.dma_start(out_blocks[b], summed[:])
+            for first in range(0, N, PIECE):
+                piece = slice(first, first + PIECE)
+                nc.vector.tensor_tensor(
+                    summed[:, piece],
+                    emb[:].indirect(offsets[:, first // 16 : (first + PIECE) // 16]),
+                    te[b][:, piece],
+                    ALU.add,
+                )
+                nc.sync.dma_start(out_blocks[b, :, piece], summed[:, piece])

@@ -40,9 +40,12 @@ def tile_cyclictisasrec_kernel(tc, table, time_seq, time_proj, offs, out):
         chunks = [[slice(first, first + CHUNK) for first in range(0, S, CHUNK)] for b in range(BLOCKS)]
         chunks[-1][-1:] = [slice(S - CHUNK, S - CHUNK // 2), slice(S - CHUNK // 2, S)]
         raw = [held.tile([P, S], F32, name=f"raw{b}") for b in range(BLOCKS)]
-        for b in range(BLOCKS):
-            for chunk in chunks[b]:
-                nc.sync.dma_start(raw[b][:, chunk], table_blocks[b, :, chunk])
+        for b in range(BLOCKS - 1):
+            for first in range(0, S, 2 * CHUNK):
+                pair = slice(first, first + 2 * CHUNK)
+                nc.sync.dma_start(raw[b][:, pair], table_blocks[b, :, pair])
+        for chunk in chunks[BLOCKS - 1]:
+            nc.sync.dma_start(raw[BLOCKS - 1][:, chunk], table_blocks[BLOCKS - 1, :, chunk])
 
         identity = held.tile([P, P], F32, name="identity")
         make_identity(nc, identity[:])

@@ -50,6 +50,10 @@ def tile_cyclictisasrec_kernel(tc, table, time_seq, time_proj, offs, out):
         identity = held.tile([P, P], F32, name="identity")
         make_identity(nc, identity[:])
 
+        warm = held.tile([WAVES, 2], F32, name="warm")
+        nc.vector.memset(warm[:], 0.0)
+        nc.scalar.activation(warm[:, 1:2], warm[:, 0:1], SIN)
+
         rate = held.tile([WAVES, 1], F32, name="rate")
         shift = held.tile([WAVES, 1], F32, name="shift")
         nc.vector.memset(rate[:], 0.0)

@@ -90,7 +90,9 @@ def tile_cyclictisasrec_kernel(tc, table, time_seq, time_proj, offs, out):
         for b in range(BLOCKS):
             emb = held.tile([P, S], F32, name=f"emb{b}")
             for q, chunk in enumerate(chunks[b]):
-                if q == 2:
+                if q == 2 and b == BLOCKS - 1:
+                    nc.vector.tensor_scalar_mul(emb[:, chunk], raw[b][:, chunk], math.sqrt(C))
+                elif q == 2:
                     nc.gpsimd.tensor_scalar(
                         emb[:, chunk], raw[b][:, chunk], math.sqrt(C), 0.0, ALU.mult, ALU.add
                     )

@@ -100,11 +100,12 @@ def tile_cyclictisasrec_kernel(tc, table, time_seq, time_proj, offs, out):
                     nc.scalar.mul(emb[:, chunk], raw[b][:, chunk], math.sqrt(C))
 
             summed = held.tile([P, N], F32, name=f"summed{b}")
-            for first in range(0, N, PIECE):
-                piece = slice(first, first + PIECE)
+            entries = PIECE // 2 if b == BLOCKS - 1 else PIECE
+            for first in range(0, N, entries):
+                piece = slice(first, first + entries)
                 nc.vector.tensor_tensor(
                     summed[:, piece],
-                    emb[:].indirect(offsets[:, first // 16 : (first + PIECE) // 16]),
+                    emb[:].indirect(offsets[:, first // 16 : (first + entries) // 16]),
                     te[b][:, piece],
                     ALU.add,
                 )

@@ -16,7 +16,7 @@ BLOCKS = C // P
 WAVES = 8
 BANK = 512
 CHUNK = 1024
-PIECE = 512
+PIECE = 256
 
 FLOPS = 2 * C * N * ROWS
 
@@ -100,7 +100,7 @@ def tile_cyclictisasrec_kernel(tc, table, time_seq, time_proj, offs, out):
                     nc.scalar.mul(emb[:, chunk], raw[b][:, chunk], math.sqrt(C))
 
             summed = held.tile([P, N], F32, name=f"summed{b}")
-            entries = PIECE // 2 if b == BLOCKS - 1 else PIECE
+            entries = PIECE if b == BLOCKS - 1 else N
             for first in range(0, N, entries):
                 piece = slice(first, first + entries)
                 nc.vector.tensor_tensor(

@@ -16,7 +16,7 @@ BLOCKS = C // P
 WAVES = 8
 BANK = 512
 CHUNK = 1024
-PIECE = 256
+PIECES = (N // 2, N // 4, N // 8, N // 8)
 
 FLOPS = 2 * C * N * ROWS
 
@@ -65,27 +65,29 @@ def tile_cyclictisasrec_kernel(tc, table, time_seq, time_proj, offs, out):
         nc.vector.memset(shift[0:K, :], 0.0)
         harmonics = held.tile([P, N], F32, name="harmonics")
         nc.gpsimd.memset(harmonics[:], 0.0)
-        nc.scalar.activation(harmonics[0:WAVES, :], stamps[:], SIN, bias=shift[:], scale=rate[:])
+        halves = [slice(first, first + BANK) for first in range(0, N, BANK)]
+        for half in halves:
+            nc.scalar.activation(harmonics[0:WAVES, half], stamps[:, half], SIN, bias=shift[:], scale=rate[:])
 
-        flipped = banks.tile([ROWS, C], F32, name="bank")
-        for b in range(BLOCKS):
-            nc.tensor.transpose(flipped[:, b * P : (b + 1) * P], proj[:, b, :], identity[:])
         weights = held.tile([P, C], F32, name="weights")
         nc.gpsimd.memset(weights[:], 0.0)
-        nc.vector.tensor_copy(weights[0:ROWS, :], flipped[:])
+        for b in range(BLOCKS):
+            flipped = banks.tile([ROWS, P], F32, name="bank")
+            nc.tensor.transpose(flipped[:], proj[:, b, :], identity[:])
+            nc.vector.tensor_copy(weights[0:ROWS, b * P : (b + 1) * P], flipped[:])
 
         te = [held.tile([P, N], F32, name=f"te{b}") for b in range(BLOCKS)]
         for b in range(BLOCKS):
-            for first in range(0, N, BANK):
+            for half in halves:
                 product = banks.tile([P, BANK], F32, name="bank")
                 nc.tensor.matmul(
                     product[:],
                     weights[:, b * P : (b + 1) * P],
-                    harmonics[:, first : first + BANK],
+                    harmonics[:, half],
                     start=True,
                     stop=True,
                 )
-                nc.vector.tensor_copy(te[b][:, first : first + BANK], product[:])
+                nc.vector.tensor_copy(te[b][:, half], product[:])
 
         for b in range(BLOCKS):
             emb = held.tile([P, S], F32, name=f"emb{b}")
@@ -100,8 +102,8 @@ def tile_cyclictisasrec_kernel(tc, table, time_seq, time_proj, offs, out):
                     nc.scalar.mul(emb[:, chunk], raw[b][:, chunk], math.sqrt(C))
 
             summed = held.tile([P, N], F32, name=f"summed{b}")
-            entries = PIECE if b == BLOCKS - 1 else N
-            for first in range(0, N, entries):
+            first = 0
+            for entries in PIECES if b == BLOCKS - 1 else (N,):
                 piece = slice(first, first + entries)
                 nc.vector.tensor_tensor(
                     summed[:, piece],
@@ -110,3 +112,4 @@ def tile_cyclictisasrec_kernel(tc, table, time_seq, time_proj, offs, out):
                     ALU.add,
                 )
                 nc.sync.dma_start(out_blocks[b, :, piece], summed[:, piece])
+                first += entries

@@ -16,7 +16,7 @@ BLOCKS = C // P
 WAVES = 8
 BANK = 512
 CHUNK = 1024
-PIECES = (N // 2, N // 4, N // 8, N // 8)
+PIECES = (N // 2, N // 4, N // 4)
 
 FLOPS = 2 * C * N * ROWS
 
@@ -25,6 +25,7 @@ def tile_cyclictisasrec_kernel(tc, table, time_seq, time_proj, offs, out):
     nc = tc.nc
     table_blocks = table.rearrange("(p b) s -> b p s", b=BLOCKS)
     out_blocks = out.rearrange("(p b) n -> b p n", b=BLOCKS)
+    out_rows = out.rearrange("(p b) n -> p b n", b=BLOCKS)
     with (
         tc.tile_pool(name="held", bufs=1) as held,
         tc.psum_pool(name="banks", bufs=8) as banks,
@@ -37,15 +38,18 @@ def tile_cyclictisasrec_kernel(tc, table, time_seq, time_proj, offs, out):
         proj = held.tile([P, BLOCKS, ROWS], F32, name="proj")
         nc.sync.dma_start(proj[:], time_proj.rearrange("(p b) r -> p b r", b=BLOCKS))
 
-        chunks = [[slice(first, first + CHUNK) for first in range(0, S, CHUNK)] for b in range(BLOCKS)]
-        chunks[-1][-1:] = [slice(S - CHUNK, S - CHUNK // 2), slice(S - CHUNK // 2, S)]
+        HALF, LAST = S // 2, S // 8
+        halves_of_block = [slice(0, HALF), slice(HALF, S)]
+        loads = [
+            halves_of_block,
+            halves_of_block,
+            halves_of_block,
+            [slice(0, HALF), slice(HALF, S - LAST), slice(S - LAST, S)],
+        ]
         raw = [held.tile([P, S], F32, name=f"raw{b}") for b in range(BLOCKS)]
-        for b in range(BLOCKS - 1):
-            for first in range(0, S, 2 * CHUNK):
-                pair = slice(first, first + 2 * CHUNK)
-                nc.sync.dma_start(raw[b][:, pair], table_blocks[b, :, pair])
-        for chunk in chunks[BLOCKS - 1]:
-            nc.sync.dma_start(raw[BLOCKS - 1][:, chunk], table_blocks[BLOCKS - 1, :, chunk])
+        for b in range(BLOCKS):
+            for columns in loads[b]:
+                nc.sync.dma_start(raw[b][:, columns], table_blocks[b, :, columns])
 
         identity = held.tile([P, P], F32, name="identity")
         make_identity(nc, identity[:])
@@ -89,19 +93,21 @@ def tile_cyclictisasrec_kernel(tc, table, time_seq, time_proj, offs, out):
                 )
                 nc.vector.tensor_copy(te[b][:, half], product[:])
 
+        pair = held.tile([P, 2, N], F32, name="pair")
         for b in range(BLOCKS):
             emb = held.tile([P, S], F32, name=f"emb{b}")
-            for q, chunk in enumerate(chunks[b]):
-                if q == 2 and b == BLOCKS - 1:
-                    nc.vector.tensor_scalar_mul(emb[:, chunk], raw[b][:, chunk], math.sqrt(C))
-                elif q == 2:
-                    nc.gpsimd.tensor_scalar(
-                        emb[:, chunk], raw[b][:, chunk], math.sqrt(C), 0.0, ALU.mult, ALU.add
-                    )
-                else:
-                    nc.scalar.mul(emb[:, chunk], raw[b][:, chunk], math.sqrt(C))
+            half, third, fourth = slice(0, HALF), slice(HALF, HALF + CHUNK), slice(HALF + CHUNK, S)
+            if b < BLOCKS - 1:
+                nc.scalar.mul(emb[:, half], raw[b][:, half], math.sqrt(C))
+                nc.gpsimd.tensor_scalar(emb[:, third], raw[b][:, third], math.sqrt(C), 0.0, ALU.mult, ALU.add)
+                nc.scalar.mul(emb[:, fourth], raw[b][:, fourth], math.sqrt(C))
+            else:
+                middle, last = loads[b][1:]
+                nc.scalar.mul(emb[:, half], raw[b][:, half], math.sqrt(C))
+                nc.vector.tensor_scalar_mul(emb[:, middle], raw[b][:, middle], math.sqrt(C))
+                nc.scalar.mul(emb[:, last], raw[b][:, last], math.sqrt(C))
 
-            summed = held.tile([P, N], F32, name=f"summed{b}")
+            summed = pair[:, b, :] if b < 2 else held.tile([P, N], F32, name=f"summed{b}")
             first = 0
             for entries in PIECES if b == BLOCKS - 1 else (N,):
                 piece = slice(first, first + entries)
@@ -111,5 +117,8 @@ def tile_cyclictisasrec_kernel(tc, table, time_seq, time_proj, offs, out):
                     te[b][:, piece],
                     ALU.add,
                 )
-                nc.sync.dma_start(out_blocks[b, :, piece], summed[:, piece])
+                if b == 1:
+                    nc.sync.dma_start(out_rows[:, 0:2, :], pair[:])
+                elif b > 1:
+                    nc.sync.dma_start(out_blocks[b, :, piece], summed[:, piece])
                 first += entries

@@ -31,8 +31,6 @@ def tile_cyclictisasrec_kernel(tc, table, time_seq, time_proj, offs, out):
         tc.psum_pool(name="banks", bufs=8) as banks,
     ):
         offsets = held.tile([P, N // 16], U16, name="offsets")
-        nc.sync.dma_start(offsets[:], offs)
-
         stamps = held.tile([WAVES, N], F32, name="stamps")
         nc.sync.dma_start(stamps[:], time_seq.rearrange("o n -> (o n)").partition_broadcast(WAVES))
         proj = held.tile([P, BLOCKS, ROWS], F32, name="proj")
@@ -50,6 +48,8 @@ def tile_cyclictisasrec_kernel(tc, table, time_seq, time_proj, offs, out):
         for b in range(BLOCKS):
             for columns in loads[b]:
                 nc.sync.dma_start(raw[b][:, columns], table_blocks[b, :, columns])
+            if b == 0:
+                nc.sync.dma_start(offsets[:], offs)
 
         identity = held.tile([P, P], F32, name="identity")
         make_identity(nc, identity[:])

import math

import concourse.mybir as mybir
from concourse.masks import make_identity

F32 = mybir.dt.float32
U16 = mybir.dt.uint16
ALU = mybir.AluOpType
SIN = mybir.ActivationFunctionType.Sin

P = 128
C, S, N, K = 512, 4096, 1024, 3
PERIODS = (86400.0, 604800.0, 2592000.0)
ROWS = 2 * K
BLOCKS = C // P
WAVES = 8
BANK = 512
CHUNK = 1024
PIECES = (N // 2, N // 4, N // 4)

FLOPS = 2 * C * N * ROWS


def tile_cyclictisasrec_kernel(tc, table, time_seq, time_proj, offs, out):
    nc = tc.nc
    table_blocks = table.rearrange("(p b) s -> b p s", b=BLOCKS)
    out_blocks = out.rearrange("(p b) n -> b p n", b=BLOCKS)
    out_rows = out.rearrange("(p b) n -> p b n", b=BLOCKS)
    with (
        tc.tile_pool(name="held", bufs=1) as held,
        tc.psum_pool(name="banks", bufs=8) as banks,
    ):
        offsets = held.tile([P, N // 16], U16, name="offsets")
        stamps = held.tile([WAVES, N], F32, name="stamps")
        nc.sync.dma_start(stamps[:], time_seq.rearrange("o n -> (o n)").partition_broadcast(WAVES))
        proj = held.tile([P, BLOCKS, ROWS], F32, name="proj")
        nc.sync.dma_start(proj[:], time_proj.rearrange("(p b) r -> p b r", b=BLOCKS))

        HALF, LAST = S // 2, S // 8
        halves_of_block = [slice(0, HALF), slice(HALF, S)]
        loads = [
            halves_of_block,
            halves_of_block,
            halves_of_block,
            [slice(0, HALF), slice(HALF, S - LAST), slice(S - LAST, S)],
        ]
        raw = [held.tile([P, S], F32, name=f"raw{b}") for b in range(BLOCKS)]
        for b in range(BLOCKS):
            for columns in loads[b]:
                nc.sync.dma_start(raw[b][:, columns], table_blocks[b, :, columns])
            if b == 0:
                nc.sync.dma_start(offsets[:], offs)

        identity = held.tile([P, P], F32, name="identity")
        make_identity(nc, identity[:])

        warm = held.tile([WAVES, 2], F32, name="warm")
        nc.vector.memset(warm[:], 0.0)
        nc.scalar.activation(warm[:, 1:2], warm[:, 0:1], SIN)

        rate = held.tile([WAVES, 1], F32, name="rate")
        shift = held.tile([WAVES, 1], F32, name="shift")
        nc.vector.memset(rate[:], 0.0)
        for r in reversed(range(ROWS)):
            turn = 2.0 * math.pi if r < K else -2.0 * math.pi
            nc.vector.memset(rate[0 : r + 1, :], turn / PERIODS[r % K])
        nc.vector.memset(shift[:], 0.0)
        nc.vector.memset(shift[0:ROWS, :], math.pi / 2.0)
        nc.vector.memset(shift[0:K, :], 0.0)
        harmonics = held.tile([P, N], F32, name="harmonics")
        nc.gpsimd.memset(harmonics[:], 0.0)
        halves = [slice(first, first + BANK) for first in range(0, N, BANK)]
        for half in halves:
            nc.scalar.activation(harmonics[0:WAVES, half], stamps[:, half], SIN, bias=shift[:], scale=rate[:])

        weights = held.tile([P, C], F32, name="weights")
        nc.gpsimd.memset(weights[:], 0.0)
        for b in range(BLOCKS):
            flipped = banks.tile([ROWS, P], F32, name="bank")
            nc.tensor.transpose(flipped[:], proj[:, b, :], identity[:])
            nc.vector.tensor_copy(weights[0:ROWS, b * P : (b + 1) * P], flipped[:])

        te = [held.tile([P, N], F32, name=f"te{b}") for b in range(BLOCKS)]
        for b in range(BLOCKS):
            for half in halves:
                product = banks.tile([P, BANK], F32, name="bank")
                nc.tensor.matmul(
                    product[:],
                    weights[:, b * P : (b + 1) * P],
                    harmonics[:, half],
                    start=True,
                    stop=True,
                )
                nc.vector.tensor_copy(te[b][:, half], product[:])

        pair = held.tile([P, 2, N], F32, name="pair")
        for b in range(BLOCKS):
            emb = held.tile([P, S], F32, name=f"emb{b}")
            half, third, fourth = slice(0, HALF), slice(HALF, HALF + CHUNK), slice(HALF + CHUNK, S)
            if b < BLOCKS - 1:
                nc.scalar.mul(emb[:, half], raw[b][:, half], math.sqrt(C))
                nc.gpsimd.tensor_scalar(emb[:, third], raw[b][:, third], math.sqrt(C), 0.0, ALU.mult, ALU.add)
                nc.scalar.mul(emb[:, fourth], raw[b][:, fourth], math.sqrt(C))
            else:
                middle, last = loads[b][1:]
                nc.scalar.mul(emb[:, half], raw[b][:, half], math.sqrt(C))
                nc.vector.tensor_scalar_mul(emb[:, middle], raw[b][:, middle], math.sqrt(C))
                nc.scalar.mul(emb[:, last], raw[b][:, last], math.sqrt(C))

            summed = pair[:, b, :] if b < 2 else held.tile([P, N], F32, name=f"summed{b}")
            first = 0
            for entries in PIECES if b == BLOCKS - 1 else (N,):
                piece = slice(first, first + entries)
                nc.vector.tensor_tensor(
                    summed[:, piece],
                    emb[:].indirect(offsets[:, first // 16 : (first + entries) // 16]),
                    te[b][:, piece],
                    ALU.add,
                )
                if b == 1:
                    nc.sync.dma_start(out_rows[:, 0:2, :], pair[:])
                elif b > 1:
                    nc.sync.dma_start(out_blocks[b, :, piece], summed[:, piece])
                first += entries
